import numpy as np
import ml_dtypes


def mxq(x, axis, fmt="e4m3"):
    dtype, down = {"e4m3": (ml_dtypes.float8_e4m3fn, 7), "e5m2": (ml_dtypes.float8_e5m2, 14)}[fmt]
    v = np.moveaxis(np.asarray(x, np.float32).astype(ml_dtypes.bfloat16).astype(np.float64), axis, -1)
    blocks = v.reshape(v.shape[:-1] + (-1, 32))
    amax = np.abs(blocks).max(-1, keepdims=True)
    byte = np.maximum(np.where(amax > 0, np.frexp(amax)[1] - 1 + 127, 0) - down, 1)
    scale = np.exp2(byte - 127.0)
    codes = (blocks / scale).astype(np.float32).astype(dtype).astype(np.float64)
    return np.moveaxis((codes * scale).reshape(v.shape), -1, axis)


WIDE = False


def mx_kscale(k):
    if not WIDE:
        return np.ones(k)
    levels = np.array([10, -10, 5, -5, 0])
    a = np.random.permutation(np.resize(levels, k // 512 * 4)).reshape(k // 512, 4)
    idx = np.arange(k)
    return np.exp2(a[idx // 512, idx % 128 // 32])


BF16 = ml_dtypes.bfloat16


def bf(x):
    return np.asarray(x, np.float32).astype(BF16)


def f64(x):
    return np.asarray(x).astype(np.float64)


B, IN_F, OUT_F = 10240, 1024, 256
EPS = 1e-5


def setup_inputs():
    s = mx_kscale(IN_F)
    scale = 1.0 / np.sqrt(IN_F)
    return {"x": bf(np.random.standard_normal((B, IN_F)) * s),
            "y": bf(np.random.standard_normal((B, OUT_F))),
            "weight": bf(np.random.uniform(-scale, scale, (OUT_F, IN_F)) / s[None, :]),
            "bias": bf(np.random.uniform(-0.5, 0.5, OUT_F)),
            "running_mean": bf(np.random.standard_normal(OUT_F) * 0.3),
            "running_var": bf(np.random.uniform(0.5, 1.5, OUT_F)),
            "norm_weight": bf(1.0 + 0.1 * np.random.standard_normal(OUT_F)),
            "norm_bias": bf(np.random.standard_normal(OUT_F) * 0.3)}


def reference(x, y, weight, bias, running_mean, running_var, norm_weight, norm_bias):
    linear = (mxq(f64(x), 1, "e4m3") @ mxq(f64(weight), 1, "e4m3").T) + f64(bias)
    inv_std = 1.0 / np.sqrt(f64(running_var) + EPS)
    norm = (linear - f64(running_mean)) * inv_std * f64(norm_weight) + f64(norm_bias)
    return (norm + f64(y)) * f64(y)

@@ -1,0 +1,215 @@
+from contextlib import ExitStack
+
+import concourse.mybir as mybir
+from concourse.masks import make_identity
+
+F32 = mybir.dt.float32
+BF16 = mybir.dt.bfloat16
+U32 = mybir.dt.uint32
+U8 = mybir.dt.uint8
+FP8X4 = mybir.dt.float8_e4m3fn_x4
+ACT = mybir.ActivationFunctionType
+ALU = mybir.AluOpType
+
+P = 128
+B, IN_F, OUT_F = 10240, 1024, 256
+EPS = 1e-5
+FLOPS = 2 * B * IN_F * OUT_F
+
+CH = 512
+NCH = B // CH
+JG = 8
+NG = B // (P * JG)
+MANUAL = True
+
+
+def tile_modelnew_t_kernel(
+    tc, x, y, weight, bias, running_mean, running_var, norm_weight, norm_bias, out
+):
+    nc = tc.nc
+    xv = x.rearrange("(g p j) k -> g p (j k)", p=P, j=JG)
+    yv = y.rearrange("(g p j) f -> g p (j f)", p=P, j=JG)
+    ov = out.rearrange("(g p j) f -> g p (j f)", p=P, j=JG)
+
+    with ExitStack() as ctx:
+        if MANUAL:
+            ctx.enter_context(tc.manual_schedule())
+        const = ctx.enter_context(tc.tile_pool(name="const", bufs=1))
+        xin = ctx.enter_context(tc.tile_pool(name="xin", bufs=4))
+        yin = ctx.enter_context(tc.tile_pool(name="yin", bufs=6))
+        work = ctx.enter_context(tc.tile_pool(name="work", bufs=3))
+        outp = ctx.enter_context(tc.tile_pool(name="outp", bufs=4))
+        xtp = ctx.enter_context(tc.psum_pool(name="xtp", bufs=4))
+        linp = ctx.enter_context(tc.psum_pool(name="linp", bufs=2))
+        nbp = ctx.enter_context(tc.psum_pool(name="nbp", bufs=2))
+
+        xs = {}
+        ys = {}
+        grps = {}
+        cods = {}
+        scls = {}
+        lins = {}
+        nts = {}
+        nbs = {}
+        outs = {}
+
+        def load(g, pieces):
+            xt = xin.tile([P, JG * IN_F], BF16, name="xs", tag="xs")
+            w = JG * IN_F // pieces
+            for s in range(pieces):
+                nc.sync.dma_start(out=xt[:, s * w:(s + 1) * w], in_=xv[g][:, s * w:(s + 1) * w])
+            yt = yin.tile([P, JG * OUT_F], BF16, name="ys", tag="ys")
+            nc.sync.dma_start(out=yt[:], in_=yv[g])
+            xs[g] = xt
+            ys[g] = yt
+
+        ident = const.tile([P, P], F32, name="ident")
+        make_identity(nc, ident[:])
+        vrows = const.tile([P, P], BF16, name="vrows")
+        nc.vector.memset(vrows[:], 0.0)
+        warm = const.tile([P, 1], F32, name="warm")
+        nc.vector.memset(warm[:], 1.0)
+        for v, vec in enumerate((bias, running_mean, running_var, norm_weight, norm_bias)):
+            nc.scalar.dma_start(out=vrows[2 * v:2 * v + 2, :], in_=vec.rearrange("(h p) -> h p", h=2))
+        warm2 = const.tile([P, 1], F32, name="warm2")
+        nc.scalar.sqrt(warm2[:], warm[:])
+
+        w_sb = const.tile([P, 2 * IN_F], BF16, name="w_sb")
+        nc.sync.dma_start(
+            out=w_sb[:].rearrange("p (h k) -> p h k", h=2),
+            in_=weight.rearrange("(h p) k -> p h k", p=P),
+        )
+        load(0, 4)
+        for g in range(1, 4):
+            load(g, 1)
+
+        w32 = w_sb[:].bitcast(F32).rearrange("p (h w) -> p h w", h=2)
+        wgrp = const.tile([P, 2048], BF16, name="wgrp", align_bytes=64)
+        wgrp32 = wgrp[:].bitcast(F32).rearrange("p (g c u) -> p g c u", g=2, u=2)
+        for g in range(2):
+            wt = xtp.tile([P, 2, 256], F32, name="wt", tag="xt")
+            for u in range(2):
+                for h in range(2):
+                    c0 = 256 * g + 128 * u
+                    nc.tensor.transpose(wt[:, u, h * P:(h + 1) * P], w32[:, h, c0:c0 + P], ident[:])
+            nc.scalar.copy(out=wgrp32[:, g], in_=wt[:].rearrange("p u c -> p c u"))
+        wcod = const.tile([P, 512], U32, name="wcod", align_bytes=64)
+        wscl = const.tile([P, 512], U8, name="wscl", align_bytes=64)
+        nc.vector.quantize_mx(out=wcod[:].bitcast(FP8X4), scales=wscl[:], in_=wgrp[:])
+
+        def stage_x(i):
+            x32 = xs[i // 2][:].bitcast(F32).rearrange("p (j w) -> p j w", j=JG)
+            grp = work.tile([P, 4096], BF16, name="grp", tag="grp", align_bytes=64)
+            grp32 = grp[:].bitcast(F32).rearrange("p (g c u) -> p g c u", g=2, u=2)
+            for jp in range(2):
+                for g in range(2):
+                    bank = xtp.tile([P, 2, 256], F32, name="xt", tag="xt")
+                    for u in range(2):
+                        for jj in range(2):
+                            j = (i % 2) * 4 + jp * 2 + jj
+                            c0 = 256 * g + 128 * u
+                            nc.tensor.transpose(bank[:, u, jj * P:(jj + 1) * P], x32[:, j, c0:c0 + P], ident[:])
+                    nc.scalar.copy(
+                        out=grp32[:, g, jp * 256:(jp + 1) * 256, :],
+                        in_=bank[:].rearrange("p u c -> p c u"),
+                    )
+            grps[i] = grp
+
+        def stage_q(i):
+            cod = work.tile([P, 1024], U32, name="cod", tag="cod", align_bytes=64)
+            scl = work.tile([P, 1024], U8, name="scl", tag="scl", align_bytes=64)
+            nc.vector.quantize_mx(out=cod[:].bitcast(FP8X4), scales=scl[:], in_=grps[i][:])
+            cods[i] = cod
+            scls[i] = scl
+
+        def stage_m(i):
+            lins[i] = []
+            for h in range(2):
+                lin = linp.tile([P, CH], F32, name="lin", tag="lin")
+                for g in range(2):
+                    w0 = g * 256 + h * P
+                    nc.tensor.matmul_mx(
+                        out=lin[:],
+                        lhsT=wcod[:, w0:w0 + P].bitcast(FP8X4),
+                        lhsT_scale=wscl[:, w0:w0 + P],
+                        rhs=cods[i][:, g * CH:(g + 1) * CH].bitcast(FP8X4),
+                        rhs_scale=scls[i][:, g * CH:(g + 1) * CH],
+                        start=(g == 0),
+                        stop=(g == 1),
+                    )
+                lins[i].append(lin)
+
+        def stage_a(i):
+            nt = work.tile([P, 2, CH], F32, name="nt", tag="nt")
+            for h in range(2):
+                nc.scalar.activation(
+                    out=nt[:, h, :], in_=lins[i][h][:], func=ACT.Identity,
+                    scale=s_col[:, h:h + 1], bias=t_col[:, h:h + 1],
+                )
+            nts[i] = nt
+
+        def stage_b(i):
+            nbs[i] = []
+            for jp in range(2):
+                nb = nbp.tile([P, 2, 256], F32, name="nb", tag="nb")
+                for jj in range(2):
+                    for h in range(2):
+                        c0 = (jp * 2 + jj) * P
+                        nc.tensor.transpose(nb[:, jj, h * P:(h + 1) * P], nts[i][:, h, c0:c0 + P], ident[:])
+                nbs[i].append(nb)
+
+        def stage_d(i):
+            o = outp.tile([P, 4 * OUT_F], F32, name="o", tag="o")
+            o3 = o[:].rearrange("p (j f) -> p j f", j=4)
+            y3 = ys[i // 2][:].rearrange("p (j f) -> p j f", j=JG)
+            for jp in range(2):
+                j0 = (i % 2) * 4 + jp * 2
+                nc.vector.tensor_tensor(
+                    out=o3[:, jp * 2:jp * 2 + 2, :], in0=nbs[i][jp][:], in1=y3[:, j0:j0 + 2, :], op=ALU.add
+                )
+            outs[i] = o
+
+        def stage_u(i):
+            o = outs[i]
+            c0 = (i % 2) * 4 * OUT_F
+            nc.vector.tensor_tensor(
+                out=o[:], in0=o[:], in1=ys[i // 2][:, c0:c0 + 4 * OUT_F], op=ALU.mult
+            )
+            nc.gpsimd.dma_start(out=ov[i // 2][:, c0:c0 + 4 * OUT_F], in_=o[:])
+
+        stage_x(0)
+
+        vrows32 = const.tile([P, P], F32, name="vrows32")
+        nc.vector.tensor_copy(out=vrows32[:], in_=vrows[:])
+        pv = nbp.tile([P, 2, 256], F32, name="pv", tag="nb")
+        nc.tensor.transpose(pv[:, 0, 0:P], vrows32[:], ident[:])
+        prm = const.tile([P, 10], F32, name="prm")
+        nc.vector.tensor_copy(out=prm[:], in_=pv[:, 0, 0:10])
+        tmp = const.tile([P, 8], F32, name="tmp")
+        s_col = const.tile([P, 2], F32, name="s_col")
+        t_col = const.tile([P, 2], F32, name="t_col")
+        nc.vector.tensor_scalar_add(out=tmp[:, 0:2], in0=prm[:, 4:6], scalar1=EPS)
+        sd = const.tile([P, 2], F32, name="sd")
+        nc.scalar.sqrt(sd[:], tmp[:, 0:2])
+        nc.vector.reciprocal(out=tmp[:, 2:4], in_=sd[:])
+        nc.vector.tensor_tensor(out=s_col[:], in0=tmp[:, 2:4], in1=prm[:, 6:8], op=ALU.mult)
+        nc.vector.tensor_tensor(out=tmp[:, 4:6], in0=prm[:, 0:2], in1=prm[:, 2:4], op=ALU.subtract)
+        nc.vector.tensor_tensor(out=tmp[:, 6:8], in0=tmp[:, 4:6], in1=s_col[:], op=ALU.mult)
+        nc.vector.tensor_tensor(out=t_col[:], in0=tmp[:, 6:8], in1=prm[:, 8:10], op=ALU.add)
+
+        for k in range(NCH + 2):
+            if 1 <= k <= NCH:
+                stage_a(k - 1)
+            if k + 1 < NCH:
+                stage_x(k + 1)
+                if (k + 1) % 2 == 1 and (k + 1) // 2 + 4 < NG:
+                    load((k + 1) // 2 + 4, 1)
+            if k < NCH:
+                stage_q(k)
+            if k >= 2:
+                stage_u(k - 2)
+            if 1 <= k <= NCH:
+                stage_b(k - 1)
+                stage_d(k - 1)
+            if k < NCH:
+                stage_m(k)

@@ -177,8 +177,6 @@ def tile_modelnew_t_kernel(
             )
             nc.gpsimd.dma_start(out=ov[i // 2][:, c0:c0 + 4 * OUT_F], in_=o[:])
 
-        stage_x(0)
-
         vrows32 = const.tile([P, P], F32, name="vrows32")
         nc.vector.tensor_copy(out=vrows32[:], in_=vrows[:])
         pv = nbp.tile([P, 2, 256], F32, name="pv", tag="nb")
@@ -197,19 +195,19 @@ def tile_modelnew_t_kernel(
         nc.vector.tensor_tensor(out=tmp[:, 6:8], in0=tmp[:, 4:6], in1=s_col[:], op=ALU.mult)
         nc.vector.tensor_tensor(out=t_col[:], in0=tmp[:, 6:8], in1=prm[:, 8:10], op=ALU.add)
 
-        for k in range(NCH + 2):
-            if 1 <= k <= NCH:
-                stage_a(k - 1)
+        stage_x(0)
+        stage_q(0)
+        for k in range(NCH + 1):
             if k + 1 < NCH:
                 stage_x(k + 1)
                 if (k + 1) % 2 == 1 and (k + 1) // 2 + 4 < NG:
                     load((k + 1) // 2 + 4, 1)
             if k < NCH:
-                stage_q(k)
-            if k >= 2:
-                stage_u(k - 2)
-            if 1 <= k <= NCH:
+                stage_m(k)
+                stage_a(k)
+            if k + 1 < NCH:
+                stage_q(k + 1)
+            if k >= 1:
                 stage_b(k - 1)
                 stage_d(k - 1)
-            if k < NCH:
-                stage_m(k)
+                stage_u(k - 1)

@@ -97,53 +97,53 @@ def tile_modelnew_t_kernel(
         wscl = const.tile([P, 512], U8, name="wscl", align_bytes=64)
         nc.vector.quantize_mx(out=wcod[:].bitcast(FP8X4), scales=wscl[:], in_=wgrp[:])
 
-        def stage_x(i):
+        def x_bank(i, b):
+            g, jp = b // 2, b % 2
+            if b == 0:
+                grps[i] = work.tile([P, 4096], BF16, name="grp", tag="grp", align_bytes=64)
             x32 = xs[i // 2][:].bitcast(F32).rearrange("p (j w) -> p j w", j=JG)
-            grp = work.tile([P, 4096], BF16, name="grp", tag="grp", align_bytes=64)
-            grp32 = grp[:].bitcast(F32).rearrange("p (g c u) -> p g c u", g=2, u=2)
-            for jp in range(2):
-                for g in range(2):
-                    bank = xtp.tile([P, 2, 256], F32, name="xt", tag="xt")
-                    for u in range(2):
-                        for jj in range(2):
-                            j = (i % 2) * 4 + jp * 2 + jj
-                            c0 = 256 * g + 128 * u
-                            nc.tensor.transpose(bank[:, u, jj * P:(jj + 1) * P], x32[:, j, c0:c0 + P], ident[:])
-                    nc.scalar.copy(
-                        out=grp32[:, g, jp * 256:(jp + 1) * 256, :],
-                        in_=bank[:].rearrange("p u c -> p c u"),
-                    )
-            grps[i] = grp
+            grp32 = grps[i][:].bitcast(F32).rearrange("p (g c u) -> p g c u", g=2, u=2)
+            bank = xtp.tile([P, 2, 256], F32, name="xt", tag="xt")
+            for u in range(2):
+                for jj in range(2):
+                    j = (i % 2) * 4 + jp * 2 + jj
+                    c0 = 256 * g + 128 * u
+                    nc.tensor.transpose(bank[:, u, jj * P:(jj + 1) * P], x32[:, j, c0:c0 + P], ident[:])
+            nc.scalar.copy(
+                out=grp32[:, g, jp * 256:(jp + 1) * 256, :],
+                in_=bank[:].rearrange("p u c -> p c u"),
+            )
 
-        def stage_q(i):
-            cod = work.tile([P, 1024], U32, name="cod", tag="cod", align_bytes=64)
-            scl = work.tile([P, 1024], U8, name="scl", tag="scl", align_bytes=64)
-            nc.vector.quantize_mx(out=cod[:].bitcast(FP8X4), scales=scl[:], in_=grps[i][:])
-            cods[i] = cod
-            scls[i] = scl
+        def stage_q(i, g):
+            if g == 0:
+                cods[i] = work.tile([P, 1024], U32, name="cod", tag="cod", align_bytes=64)
+                scls[i] = work.tile([P, 1024], U8, name="scl", tag="scl", align_bytes=64)
+            nc.vector.quantize_mx(
+                out=cods[i][:, g * CH:(g + 1) * CH].bitcast(FP8X4),
+                scales=scls[i][:, g * CH:(g + 1) * CH],
+                in_=grps[i][:, g * 2048:(g + 1) * 2048],
+            )
 
-        def stage_m(i):
-            lins[i] = []
-            for h in range(2):
-                lin = linp.tile([P, CH], F32, name="lin", tag="lin")
-                for g in range(2):
-                    w0 = g * 256 + h * P
-                    nc.tensor.matmul_mx(
-                        out=lin[:],
-                        lhsT=wcod[:, w0:w0 + P].bitcast(FP8X4),
-                        lhsT_scale=wscl[:, w0:w0 + P],
-                        rhs=cods[i][:, g * CH:(g + 1) * CH].bitcast(FP8X4),
-                        rhs_scale=scls[i][:, g * CH:(g + 1) * CH],
-                        start=(g == 0),
-                        stop=(g == 1),
-                    )
-                lins[i].append(lin)
+        def stage_m(i, h):
+            lin = linp.tile([P, CH], F32, name="lin", tag="lin")
+            for g in range(2):
+                w0 = g * 256 + h * P
+                nc.tensor.matmul_mx(
+                    out=lin[:],
+                    lhsT=wcod[:, w0:w0 + P].bitcast(FP8X4),
+                    lhsT_scale=wscl[:, w0:w0 + P],
+                    rhs=cods[i][:, g * CH:(g + 1) * CH].bitcast(FP8X4),
+                    rhs_scale=scls[i][:, g * CH:(g + 1) * CH],
+                    start=(g == 0),
+                    stop=(g == 1),
+                )
+            lins[(i, h)] = lin
 
         def stage_a(i):
             nt = work.tile([P, 2, CH], F32, name="nt", tag="nt")
             for h in range(2):
                 nc.scalar.activation(
-                    out=nt[:, h, :], in_=lins[i][h][:], func=ACT.Identity,
+                    out=nt[:, h, :], in_=lins[(i, h)][:], func=ACT.Identity,
                     scale=s_col[:, h:h + 1], bias=t_col[:, h:h + 1],
                 )
             nts[i] = nt
@@ -195,19 +195,28 @@ def tile_modelnew_t_kernel(
         nc.vector.tensor_tensor(out=tmp[:, 6:8], in0=tmp[:, 4:6], in1=s_col[:], op=ALU.mult)
         nc.vector.tensor_tensor(out=t_col[:], in0=tmp[:, 6:8], in1=prm[:, 8:10], op=ALU.add)
 
-        stage_x(0)
-        stage_q(0)
+        for b in range(4):
+            x_bank(0, b)
+        stage_q(0, 0)
+        stage_q(0, 1)
         for k in range(NCH + 1):
-            if k + 1 < NCH:
-                stage_x(k + 1)
+            nxt = k + 1 < NCH
+            if nxt:
+                for b in range(3):
+                    x_bank(k + 1, b)
+            if k < NCH:
+                stage_m(k, 0)
+            if nxt:
+                x_bank(k + 1, 3)
                 if (k + 1) % 2 == 1 and (k + 1) // 2 + 4 < NG:
                     load((k + 1) // 2 + 4, 1)
-            if k < NCH:
-                stage_m(k)
-                stage_a(k)
-            if k + 1 < NCH:
-                stage_q(k + 1)
+                stage_q(k + 1, 0)
+                stage_q(k + 1, 1)
             if k >= 1:
                 stage_b(k - 1)
+            if k < NCH:
+                stage_m(k, 1)
+                stage_a(k)
+            if k >= 1:
                 stage_d(k - 1)
                 stage_u(k - 1)

@@ -175,7 +175,7 @@ def tile_modelnew_t_kernel(
             nc.vector.tensor_tensor(
                 out=o[:], in0=o[:], in1=ys[i // 2][:, c0:c0 + 4 * OUT_F], op=ALU.mult
             )
-            nc.gpsimd.dma_start(out=ov[i // 2][:, c0:c0 + 4 * OUT_F], in_=o[:])
+            nc.sync.dma_start(out=ov[i // 2][:, c0:c0 + 4 * OUT_F], in_=o[:])
 
         vrows32 = const.tile([P, P], F32, name="vrows32")
         nc.vector.tensor_copy(out=vrows32[:], in_=vrows[:])

@@ -38,7 +38,7 @@ def tile_modelnew_t_kernel(
         xin = ctx.enter_context(tc.tile_pool(name="xin", bufs=4))
         yin = ctx.enter_context(tc.tile_pool(name="yin", bufs=6))
         work = ctx.enter_context(tc.tile_pool(name="work", bufs=3))
-        outp = ctx.enter_context(tc.tile_pool(name="outp", bufs=4))
+        outp = ctx.enter_context(tc.tile_pool(name="outp", bufs=10))
         xtp = ctx.enter_context(tc.psum_pool(name="xtp", bufs=4))
         linp = ctx.enter_context(tc.psum_pool(name="linp", bufs=2))
         nbp = ctx.enter_context(tc.psum_pool(name="nbp", bufs=2))

@@ -53,14 +53,16 @@ def tile_modelnew_t_kernel(
         nbs = {}
         outs = {}
 
-        def load(g, pieces):
+        def load_x(g, pieces):
             xt = xin.tile([P, JG * IN_F], BF16, name="xs", tag="xs")
             w = JG * IN_F // pieces
             for s in range(pieces):
                 nc.sync.dma_start(out=xt[:, s * w:(s + 1) * w], in_=xv[g][:, s * w:(s + 1) * w])
+            xs[g] = xt
+
+        def load_y(g):
             yt = yin.tile([P, JG * OUT_F], BF16, name="ys", tag="ys")
             nc.sync.dma_start(out=yt[:], in_=yv[g])
-            xs[g] = xt
             ys[g] = yt
 
         ident = const.tile([P, P], F32, name="ident")
@@ -79,9 +81,13 @@ def tile_modelnew_t_kernel(
             out=w_sb[:].rearrange("p (h k) -> p h k", h=2),
             in_=weight.rearrange("(h p) k -> p h k", p=P),
         )
-        load(0, 4)
-        for g in range(1, 4):
-            load(g, 1)
+        load_x(0, 4)
+        load_x(1, 2)
+        load_y(0)
+        load_x(2, 1)
+        load_y(1)
+        load_x(3, 1)
+        load_y(2)
 
         w32 = w_sb[:].bitcast(F32).rearrange("p (h w) -> p h w", h=2)
         wgrp = const.tile([P, 2048], BF16, name="wgrp", align_bytes=64)
@@ -158,24 +164,23 @@ def tile_modelnew_t_kernel(
                         nc.tensor.transpose(nb[:, jj, h * P:(h + 1) * P], nts[i][:, h, c0:c0 + P], ident[:])
                 nbs[i].append(nb)
 
-        def stage_d(i):
-            o = outp.tile([P, 4 * OUT_F], F32, name="o", tag="o")
-            o3 = o[:].rearrange("p (j f) -> p j f", j=4)
+        def stage_d(i, jp):
+            if jp == 0:
+                outs[i] = outp.tile([P, 4 * OUT_F], F32, name="o", tag="o")
+            o3 = outs[i][:].rearrange("p (j f) -> p j f", j=4)
             y3 = ys[i // 2][:].rearrange("p (j f) -> p j f", j=JG)
-            for jp in range(2):
-                j0 = (i % 2) * 4 + jp * 2
-                nc.vector.tensor_tensor(
-                    out=o3[:, jp * 2:jp * 2 + 2, :], in0=nbs[i][jp][:], in1=y3[:, j0:j0 + 2, :], op=ALU.add
-                )
-            outs[i] = o
-
-        def stage_u(i):
-            o = outs[i]
-            c0 = (i % 2) * 4 * OUT_F
+            j0 = (i % 2) * 4 + jp * 2
             nc.vector.tensor_tensor(
-                out=o[:], in0=o[:], in1=ys[i // 2][:, c0:c0 + 4 * OUT_F], op=ALU.mult
+                out=o3[:, jp * 2:jp * 2 + 2, :], in0=nbs[i][jp][:], in1=y3[:, j0:j0 + 2, :], op=ALU.add
             )
-            nc.sync.dma_start(out=ov[i // 2][:, c0:c0 + 4 * OUT_F], in_=o[:])
+
+        def stage_u(i, lo, n):
+            o = outs[i]
+            c0 = (i % 2) * 4 * OUT_F + lo
+            nc.vector.tensor_tensor(
+                out=o[:, lo:lo + n], in0=o[:, lo:lo + n], in1=ys[i // 2][:, c0:c0 + n], op=ALU.mult
+            )
+            nc.sync.dma_start(out=ov[i // 2][:, c0:c0 + n], in_=o[:, lo:lo + n])
 
         vrows32 = const.tile([P, P], F32, name="vrows32")
         nc.vector.tensor_copy(out=vrows32[:], in_=vrows[:])
@@ -202,21 +207,28 @@ def tile_modelnew_t_kernel(
         for k in range(NCH + 1):
             nxt = k + 1 < NCH
             if nxt:
-                for b in range(3):
+                for b in range(4):
                     x_bank(k + 1, b)
+                g_new = (k + 1) // 2 + 4
+                if (k + 1) % 2 == 1 and g_new < NG:
+                    load_x(g_new, 1)
+                    load_y(g_new - 1)
+                    if g_new == NG - 1:
+                        load_y(g_new)
             if k < NCH:
                 stage_m(k, 0)
+                stage_m(k, 1)
+                stage_a(k)
             if nxt:
-                x_bank(k + 1, 3)
-                if (k + 1) % 2 == 1 and (k + 1) // 2 + 4 < NG:
-                    load((k + 1) // 2 + 4, 1)
                 stage_q(k + 1, 0)
                 stage_q(k + 1, 1)
             if k >= 1:
                 stage_b(k - 1)
-            if k < NCH:
-                stage_m(k, 1)
-                stage_a(k)
-            if k >= 1:
-                stage_d(k - 1)
-                stage_u(k - 1)
+                if k - 1 == NCH - 1:
+                    for jp in range(2):
+                        stage_d(k - 1, jp)
+                        stage_u(k - 1, jp * 512, 512)
+                else:
+                    stage_d(k - 1, 0)
+                    stage_d(k - 1, 1)
+                    stage_u(k - 1, 0, 1024)

@@ -180,7 +180,10 @@ def tile_modelnew_t_kernel(
             nc.vector.tensor_tensor(
                 out=o[:, lo:lo + n], in0=o[:, lo:lo + n], in1=ys[i // 2][:, c0:c0 + n], op=ALU.mult
             )
-            nc.sync.dma_start(out=ov[i // 2][:, c0:c0 + n], in_=o[:, lo:lo + n])
+
+        def stage_st(i, lo, n):
+            c0 = (i % 2) * 4 * OUT_F + lo
+            nc.sync.dma_start(out=ov[i // 2][:, c0:c0 + n], in_=outs[i][:, lo:lo + n])
 
         vrows32 = const.tile([P, P], F32, name="vrows32")
         nc.vector.tensor_copy(out=vrows32[:], in_=vrows[:])
@@ -225,10 +228,14 @@ def tile_modelnew_t_kernel(
             if k >= 1:
                 stage_b(k - 1)
                 if k - 1 == NCH - 1:
+                    stage_d(k - 1, 0)
+                    stage_d(k - 1, 1)
                     for jp in range(2):
-                        stage_d(k - 1, jp)
                         stage_u(k - 1, jp * 512, 512)
+                        stage_st(k - 1, jp * 512, 512)
                 else:
                     stage_d(k - 1, 0)
                     stage_d(k - 1, 1)
-                    stage_u(k - 1, 0, 1024)
+                    stage_u(k - 1, 0, 512)
+                    stage_u(k - 1, 512, 512)
+                    stage_st(k - 1, 0, 1024)

@@ -16,226 +16,228 @@ B, IN_F, OUT_F = 10240, 1024, 256
 EPS = 1e-5
 FLOPS = 2 * B * IN_F * OUT_F
 
-CH = 512
-NCH = B // CH
-JG = 8
-NG = B // (P * JG)
-MANUAL = True
+PASSES = IN_F // (4 * P)
+HALVES = OUT_F // P
+GROUP_TILES = 8
+GROUPS = B // (P * GROUP_TILES)
+X_BUFS = 4
+CHUNKS_OF_GROUP = (4, 4)
+CHUNKS_OF_LAST_GROUP = (4, 2, 1, 1)
+
+
+def chunk_list():
+    chunks = []
+    for g in range(GROUPS):
+        first = 0
+        for tiles in CHUNKS_OF_LAST_GROUP if g == GROUPS - 1 else CHUNKS_OF_GROUP:
+            chunks.append((g, first, tiles))
+            first += tiles
+    return chunks
 
 
 def tile_modelnew_t_kernel(
     tc, x, y, weight, bias, running_mean, running_var, norm_weight, norm_bias, out
 ):
     nc = tc.nc
-    xv = x.rearrange("(g p j) k -> g p (j k)", p=P, j=JG)
-    yv = y.rearrange("(g p j) f -> g p (j f)", p=P, j=JG)
-    ov = out.rearrange("(g p j) f -> g p (j f)", p=P, j=JG)
+    chunks = chunk_list()
+    xv = x.rearrange("(g p t) k -> g p (t k)", p=P, t=GROUP_TILES)
+    yv = y.rearrange("(g p t) f -> g p (t f)", p=P, t=GROUP_TILES)
+    ov = out.rearrange("(g p t) f -> g p (t f)", p=P, t=GROUP_TILES)
 
     with ExitStack() as ctx:
-        if MANUAL:
-            ctx.enter_context(tc.manual_schedule())
+        ctx.enter_context(tc.manual_schedule())
         const = ctx.enter_context(tc.tile_pool(name="const", bufs=1))
-        xin = ctx.enter_context(tc.tile_pool(name="xin", bufs=4))
-        yin = ctx.enter_context(tc.tile_pool(name="yin", bufs=6))
+        xin = ctx.enter_context(tc.tile_pool(name="xin", bufs=X_BUFS))
+        yin = ctx.enter_context(tc.tile_pool(name="yin", bufs=X_BUFS + 2))
         work = ctx.enter_context(tc.tile_pool(name="work", bufs=3))
         outp = ctx.enter_context(tc.tile_pool(name="outp", bufs=10))
         xtp = ctx.enter_context(tc.psum_pool(name="xtp", bufs=4))
         linp = ctx.enter_context(tc.psum_pool(name="linp", bufs=2))
         nbp = ctx.enter_context(tc.psum_pool(name="nbp", bufs=2))
 
-        xs = {}
-        ys = {}
-        grps = {}
-        cods = {}
-        scls = {}
-        lins = {}
-        nts = {}
-        nbs = {}
-        outs = {}
+        xs, ys = {}, {}
+        grouped, codes, scales, products, norm_t, norm_b, results = {}, {}, {}, {}, {}, {}, {}
 
         def load_x(g, pieces):
-            xt = xin.tile([P, JG * IN_F], BF16, name="xs", tag="xs")
-            w = JG * IN_F // pieces
+            xs[g] = xin.tile([P, GROUP_TILES * IN_F], BF16, name="xs", tag="xs")
+            w = GROUP_TILES * IN_F // pieces
             for s in range(pieces):
-                nc.sync.dma_start(out=xt[:, s * w:(s + 1) * w], in_=xv[g][:, s * w:(s + 1) * w])
-            xs[g] = xt
+                nc.sync.dma_start(out=xs[g][:, s * w:(s + 1) * w], in_=xv[g][:, s * w:(s + 1) * w])
 
         def load_y(g):
-            yt = yin.tile([P, JG * OUT_F], BF16, name="ys", tag="ys")
-            nc.sync.dma_start(out=yt[:], in_=yv[g])
-            ys[g] = yt
+            ys[g] = yin.tile([P, GROUP_TILES * OUT_F], BF16, name="ys", tag="ys")
+            nc.sync.dma_start(out=ys[g][:], in_=yv[g])
 
         ident = const.tile([P, P], F32, name="ident")
         make_identity(nc, ident[:])
-        vrows = const.tile([P, P], BF16, name="vrows")
-        nc.vector.memset(vrows[:], 0.0)
-        warm = const.tile([P, 1], F32, name="warm")
-        nc.vector.memset(warm[:], 1.0)
+        vec_rows = const.tile([P, P], BF16, name="vec_rows")
+        nc.vector.memset(vec_rows[:], 0.0)
+        one = const.tile([P, 1], F32, name="one")
+        nc.vector.memset(one[:], 1.0)
         for v, vec in enumerate((bias, running_mean, running_var, norm_weight, norm_bias)):
-            nc.scalar.dma_start(out=vrows[2 * v:2 * v + 2, :], in_=vec.rearrange("(h p) -> h p", h=2))
-        warm2 = const.tile([P, 1], F32, name="warm2")
-        nc.scalar.sqrt(warm2[:], warm[:])
+            nc.scalar.dma_start(
+                out=vec_rows[HALVES * v:HALVES * (v + 1), :], in_=vec.rearrange("(h p) -> h p", h=HALVES)
+            )
+        root_of_one = const.tile([P, 1], F32, name="root_of_one")
+        nc.scalar.sqrt(root_of_one[:], one[:])
 
-        w_sb = const.tile([P, 2 * IN_F], BF16, name="w_sb")
+        w_sb = const.tile([P, HALVES * IN_F], BF16, name="w_sb")
         nc.sync.dma_start(
-            out=w_sb[:].rearrange("p (h k) -> p h k", h=2),
+            out=w_sb[:].rearrange("p (h k) -> p h k", h=HALVES),
             in_=weight.rearrange("(h p) k -> p h k", p=P),
         )
         load_x(0, 4)
         load_x(1, 2)
         load_y(0)
-        load_x(2, 1)
-        load_y(1)
-        load_x(3, 1)
-        load_y(2)
+        for g in range(2, X_BUFS):
+            load_x(g, 1)
+            load_y(g - 1)
 
-        w32 = w_sb[:].bitcast(F32).rearrange("p (h w) -> p h w", h=2)
-        wgrp = const.tile([P, 2048], BF16, name="wgrp", align_bytes=64)
-        wgrp32 = wgrp[:].bitcast(F32).rearrange("p (g c u) -> p g c u", g=2, u=2)
-        for g in range(2):
-            wt = xtp.tile([P, 2, 256], F32, name="wt", tag="xt")
+        def transpose_words(bank, words, tiles_of_words, c):
             for u in range(2):
-                for h in range(2):
-                    c0 = 256 * g + 128 * u
-                    nc.tensor.transpose(wt[:, u, h * P:(h + 1) * P], w32[:, h, c0:c0 + P], ident[:])
-            nc.scalar.copy(out=wgrp32[:, g], in_=wt[:].rearrange("p u c -> p c u"))
-        wcod = const.tile([P, 512], U32, name="wcod", align_bytes=64)
-        wscl = const.tile([P, 512], U8, name="wscl", align_bytes=64)
-        nc.vector.quantize_mx(out=wcod[:].bitcast(FP8X4), scales=wscl[:], in_=wgrp[:])
+                for n, t in enumerate(tiles_of_words):
+                    w0 = 256 * c + P * u
+                    nc.tensor.transpose(bank[:, u, n * P:(n + 1) * P], words[:, t, w0:w0 + P], ident[:])
 
-        def x_bank(i, b):
-            g, jp = b // 2, b % 2
-            if b == 0:
-                grps[i] = work.tile([P, 4096], BF16, name="grp", tag="grp", align_bytes=64)
-            x32 = xs[i // 2][:].bitcast(F32).rearrange("p (j w) -> p j w", j=JG)
-            grp32 = grps[i][:].bitcast(F32).rearrange("p (g c u) -> p g c u", g=2, u=2)
-            bank = xtp.tile([P, 2, 256], F32, name="xt", tag="xt")
-            for u in range(2):
-                for jj in range(2):
-                    j = (i % 2) * 4 + jp * 2 + jj
-                    c0 = 256 * g + 128 * u
-                    nc.tensor.transpose(bank[:, u, jj * P:(jj + 1) * P], x32[:, j, c0:c0 + P], ident[:])
-            nc.scalar.copy(
-                out=grp32[:, g, jp * 256:(jp + 1) * 256, :],
-                in_=bank[:].rearrange("p u c -> p c u"),
+
+        w_words = w_sb[:].bitcast(F32).rearrange("p (h w) -> p h w", h=HALVES)
+        w_grouped = const.tile([P, PASSES * OUT_F * 4], BF16, name="w_grouped", align_bytes=64)
+        w_grouped_words = w_grouped[:].bitcast(F32).rearrange("p (c f u) -> p c f u", c=PASSES, u=2)
+        for c in range(PASSES):
+            bank = xtp.tile([P, 2, 256], F32, name="wt", tag="xt")
+            transpose_words(bank, w_words, range(HALVES), c)
+            nc.vector.tensor_copy(out=w_grouped_words[:, c], in_=bank[:].rearrange("p u f -> p f u"))
+        vec_rows32 = const.tile([P, P], F32, name="vec_rows32")
+        nc.vector.tensor_copy(out=vec_rows32[:], in_=vec_rows[:])
+        w_codes = const.tile([P, PASSES * OUT_F], U32, name="w_codes", align_bytes=64)
+        w_scales = const.tile([P, PASSES * OUT_F], U8, name="w_scales", align_bytes=64)
+        nc.vector.quantize_mx(out=w_codes[:].bitcast(FP8X4), scales=w_scales[:], in_=w_grouped[:])
+
+        vec_cols_ps = nbp.tile([P, 2, 256], F32, name="vec_cols_ps", tag="nb")
+        nc.tensor.transpose(vec_cols_ps[:, 0, 0:P], vec_rows32[:], ident[:])
+        cols = const.tile([P, 5 * HALVES], F32, name="cols")
+        nc.vector.tensor_copy(out=cols[:], in_=vec_cols_ps[:, 0, 0:5 * HALVES])
+        bias_c, mean_c, var_c, gain_c, shift_c = [cols[:, HALVES * v:HALVES * (v + 1)] for v in range(5)]
+        var_eps = const.tile([P, HALVES], F32, name="var_eps")
+        std = const.tile([P, HALVES], F32, name="std")
+        inv_std = const.tile([P, HALVES], F32, name="inv_std")
+        centred = const.tile([P, HALVES], F32, name="centred")
+        s_col = const.tile([P, HALVES], F32, name="s_col")
+        t_col = const.tile([P, HALVES], F32, name="t_col")
+        nc.vector.tensor_scalar_add(out=var_eps[:], in0=var_c, scalar1=EPS)
+        nc.scalar.sqrt(std[:], var_eps[:])
+        nc.vector.reciprocal(out=inv_std[:], in_=std[:])
+        nc.vector.tensor_tensor(out=s_col[:], in0=inv_std[:], in1=gain_c, op=ALU.mult)
+        nc.vector.tensor_tensor(out=centred[:], in0=bias_c, in1=mean_c, op=ALU.subtract)
+        nc.vector.tensor_tensor(out=centred[:], in0=centred[:], in1=s_col[:], op=ALU.mult)
+        nc.vector.tensor_tensor(out=t_col[:], in0=centred[:], in1=shift_c, op=ALU.add)
+
+
+        def transpose_x(i):
+            g, first, n = chunks[i]
+            words = xs[g][:].bitcast(F32).rearrange("p (t w) -> p t w", t=GROUP_TILES)
+            grouped[i] = work.tile([P, PASSES * 512 * 4], BF16, name="grouped", tag="grouped", align_bytes=64)
+            grouped_words = (
+                grouped[i][:, 0:PASSES * n * P * 4].bitcast(F32).rearrange("p (c r u) -> p c r u", c=PASSES, u=2)
             )
+            for c in range(PASSES):
+                for t0 in range(0, n, 2):
+                    in_bank = min(2, n - t0)
+                    bank = xtp.tile([P, 2, 256], F32, name="xt", tag="xt")
+                    transpose_words(bank, words, range(first + t0, first + t0 + in_bank), c)
+                    nc.scalar.copy(
+                        out=grouped_words[:, c, t0 * P:(t0 + in_bank) * P, :],
+                        in_=bank[:, :, 0:in_bank * P].rearrange("p u r -> p r u"),
+                    )
 
-        def stage_q(i, g):
-            if g == 0:
-                cods[i] = work.tile([P, 1024], U32, name="cod", tag="cod", align_bytes=64)
-                scls[i] = work.tile([P, 1024], U8, name="scl", tag="scl", align_bytes=64)
-            nc.vector.quantize_mx(
-                out=cods[i][:, g * CH:(g + 1) * CH].bitcast(FP8X4),
-                scales=scls[i][:, g * CH:(g + 1) * CH],
-                in_=grps[i][:, g * 2048:(g + 1) * 2048],
-            )
-
-        def stage_m(i, h):
-            lin = linp.tile([P, CH], F32, name="lin", tag="lin")
-            for g in range(2):
-                w0 = g * 256 + h * P
-                nc.tensor.matmul_mx(
-                    out=lin[:],
-                    lhsT=wcod[:, w0:w0 + P].bitcast(FP8X4),
-                    lhsT_scale=wscl[:, w0:w0 + P],
-                    rhs=cods[i][:, g * CH:(g + 1) * CH].bitcast(FP8X4),
-                    rhs_scale=scls[i][:, g * CH:(g + 1) * CH],
-                    start=(g == 0),
-                    stop=(g == 1),
+        def quantise_x(i):
+            n = chunks[i][2]
+            codes[i] = work.tile([P, PASSES * 512], U32, name="codes", tag="codes", align_bytes=64)
+            scales[i] = work.tile([P, PASSES * 512], U8, name="scales", tag="scales", align_bytes=64)
+            for c in range(PASSES):
+                r = slice(c * n * P, (c + 1) * n * P)
+                nc.vector.quantize_mx(
+                    out=codes[i][:, r].bitcast(FP8X4),
+                    scales=scales[i][:, r],
+                    in_=grouped[i][:, c * n * P * 4:(c + 1) * n * P * 4],
                 )
-            lins[(i, h)] = lin
 
-        def stage_a(i):
-            nt = work.tile([P, 2, CH], F32, name="nt", tag="nt")
-            for h in range(2):
+        def multiply(i):
+            n = chunks[i][2]
+            products[i] = []
+            for h in range(HALVES):
+                acc = linp.tile([P, 512], F32, name="acc", tag="acc")
+                for c in range(PASSES):
+                    f = slice(c * OUT_F + h * P, c * OUT_F + (h + 1) * P)
+                    r = slice(c * n * P, (c + 1) * n * P)
+                    nc.tensor.matmul_mx(
+                        out=acc[:, 0:n * P],
+                        lhsT=w_codes[:, f].bitcast(FP8X4),
+                        lhsT_scale=w_scales[:, f],
+                        rhs=codes[i][:, r].bitcast(FP8X4),
+                        rhs_scale=scales[i][:, r],
+                        start=(c == 0),
+                        stop=(c == PASSES - 1),
+                    )
+                products[i].append(acc)
+
+        def normalise(i):
+            n = chunks[i][2]
+            norm_t[i] = work.tile([P, HALVES, 512], F32, name="norm_t", tag="norm_t")
+            for h in range(HALVES):
                 nc.scalar.activation(
-                    out=nt[:, h, :], in_=lins[(i, h)][:], func=ACT.Identity,
+                    out=norm_t[i][:, h, 0:n * P], in_=products[i][h][:, 0:n * P], func=ACT.Identity,
                     scale=s_col[:, h:h + 1], bias=t_col[:, h:h + 1],
                 )
-            nts[i] = nt
 
-        def stage_b(i):
-            nbs[i] = []
-            for jp in range(2):
-                nb = nbp.tile([P, 2, 256], F32, name="nb", tag="nb")
-                for jj in range(2):
-                    for h in range(2):
-                        c0 = (jp * 2 + jj) * P
-                        nc.tensor.transpose(nb[:, jj, h * P:(h + 1) * P], nts[i][:, h, c0:c0 + P], ident[:])
-                nbs[i].append(nb)
+        def transpose_back(i):
+            n = chunks[i][2]
+            norm_b[i] = []
+            for t in range(n):
+                if t % 2 == 0:
+                    norm_b[i].append(nbp.tile([P, 512], F32, name="nb", tag="nb"))
+                for h in range(HALVES):
+                    f0 = (t % 2) * OUT_F + h * P
+                    nc.tensor.transpose(norm_b[i][-1][:, f0:f0 + P], norm_t[i][:, h, t * P:(t + 1) * P], ident[:])
 
-        def stage_d(i, jp):
-            if jp == 0:
-                outs[i] = outp.tile([P, 4 * OUT_F], F32, name="o", tag="o")
-            o3 = outs[i][:].rearrange("p (j f) -> p j f", j=4)
-            y3 = ys[i // 2][:].rearrange("p (j f) -> p j f", j=JG)
-            j0 = (i % 2) * 4 + jp * 2
-            nc.vector.tensor_tensor(
-                out=o3[:, jp * 2:jp * 2 + 2, :], in0=nbs[i][jp][:], in1=y3[:, j0:j0 + 2, :], op=ALU.add
-            )
+        def finish(i):
+            g, first, n = chunks[i]
+            results[i] = outp.tile([P, 4 * OUT_F], F32, name="res", tag="res")
+            res = results[i]
+            half = n * OUT_F // 2
+            y0 = first * OUT_F
+            for q in range(2):
+                lo = q * half
+                nc.vector.tensor_tensor(
+                    out=res[:, lo:lo + half],
+                    in0=norm_b[i][lo // 512][:, lo % 512:lo % 512 + half],
+                    in1=ys[g][:, y0 + lo:y0 + lo + half],
+                    op=ALU.add,
+                )
+            for q in range(2):
+                lo = q * half
+                nc.vector.tensor_tensor(
+                    out=res[:, lo:lo + half], in0=res[:, lo:lo + half], in1=ys[g][:, y0 + lo:y0 + lo + half],
+                    op=ALU.mult,
+                )
+            nc.sync.dma_start(out=ov[g][:, y0:y0 + n * OUT_F], in_=res[:, 0:n * OUT_F])
 
-        def stage_u(i, lo, n):
-            o = outs[i]
-            c0 = (i % 2) * 4 * OUT_F + lo
-            nc.vector.tensor_tensor(
-                out=o[:, lo:lo + n], in0=o[:, lo:lo + n], in1=ys[i // 2][:, c0:c0 + n], op=ALU.mult
-            )
-
-        def stage_st(i, lo, n):
-            c0 = (i % 2) * 4 * OUT_F + lo
-            nc.sync.dma_start(out=ov[i // 2][:, c0:c0 + n], in_=outs[i][:, lo:lo + n])
-
-        vrows32 = const.tile([P, P], F32, name="vrows32")
-        nc.vector.tensor_copy(out=vrows32[:], in_=vrows[:])
-        pv = nbp.tile([P, 2, 256], F32, name="pv", tag="nb")
-        nc.tensor.transpose(pv[:, 0, 0:P], vrows32[:], ident[:])
-        prm = const.tile([P, 10], F32, name="prm")
-        nc.vector.tensor_copy(out=prm[:], in_=pv[:, 0, 0:10])
-        tmp = const.tile([P, 8], F32, name="tmp")
-        s_col = const.tile([P, 2], F32, name="s_col")
-        t_col = const.tile([P, 2], F32, name="t_col")
-        nc.vector.tensor_scalar_add(out=tmp[:, 0:2], in0=prm[:, 4:6], scalar1=EPS)
-        sd = const.tile([P, 2], F32, name="sd")
-        nc.scalar.sqrt(sd[:], tmp[:, 0:2])
-        nc.vector.reciprocal(out=tmp[:, 2:4], in_=sd[:])
-        nc.vector.tensor_tensor(out=s_col[:], in0=tmp[:, 2:4], in1=prm[:, 6:8], op=ALU.mult)
-        nc.vector.tensor_tensor(out=tmp[:, 4:6], in0=prm[:, 0:2], in1=prm[:, 2:4], op=ALU.subtract)
-        nc.vector.tensor_tensor(out=tmp[:, 6:8], in0=tmp[:, 4:6], in1=s_col[:], op=ALU.mult)
-        nc.vector.tensor_tensor(out=t_col[:], in0=tmp[:, 6:8], in1=prm[:, 8:10], op=ALU.add)
-
-        for b in range(4):
-            x_bank(0, b)
-        stage_q(0, 0)
-        stage_q(0, 1)
-        for k in range(NCH + 1):
-            nxt = k + 1 < NCH
-            if nxt:
-                for b in range(4):
-                    x_bank(k + 1, b)
-                g_new = (k + 1) // 2 + 4
-                if (k + 1) % 2 == 1 and g_new < NG:
-                    load_x(g_new, 1)
-                    load_y(g_new - 1)
-                    if g_new == NG - 1:
-                        load_y(g_new)
-            if k < NCH:
-                stage_m(k, 0)
-                stage_m(k, 1)
-                stage_a(k)
-            if nxt:
-                stage_q(k + 1, 0)
-                stage_q(k + 1, 1)
+        transpose_x(0)
+        quantise_x(0)
+        for k in range(len(chunks) + 1):
+            if k + 1 < len(chunks):
+                transpose_x(k + 1)
+                g, first, n = chunks[k + 1]
+                if first + n == GROUP_TILES and g + X_BUFS < GROUPS:
+                    load_x(g + X_BUFS, 1)
+                    load_y(g + X_BUFS - 1)
+                    if g + X_BUFS == GROUPS - 1:
+                        load_y(GROUPS - 1)
+            if k < len(chunks):
+                multiply(k)
+                normalise(k)
+            if k + 1 < len(chunks):
+                quantise_x(k + 1)
             if k >= 1:
-                stage_b(k - 1)
-                if k - 1 == NCH - 1:
-                    stage_d(k - 1, 0)
-                    stage_d(k - 1, 1)
-                    for jp in range(2):
-                        stage_u(k - 1, jp * 512, 512)
-                        stage_st(k - 1, jp * 512, 512)
-                else:
-                    stage_d(k - 1, 0)
-                    stage_d(k - 1, 1)
-                    stage_u(k - 1, 0, 512)
-                    stage_u(k - 1, 512, 512)
-                    stage_st(k - 1, 0, 1024)
+                transpose_back(k - 1)
+                finish(k - 1)

from contextlib import ExitStack

import concourse.mybir as mybir
from concourse.masks import make_identity

F32 = mybir.dt.float32
BF16 = mybir.dt.bfloat16
U32 = mybir.dt.uint32
U8 = mybir.dt.uint8
FP8X4 = mybir.dt.float8_e4m3fn_x4
ACT = mybir.ActivationFunctionType
ALU = mybir.AluOpType

P = 128
B, IN_F, OUT_F = 10240, 1024, 256
EPS = 1e-5
FLOPS = 2 * B * IN_F * OUT_F

PASSES = IN_F // (4 * P)
HALVES = OUT_F // P
GROUP_TILES = 8
GROUPS = B // (P * GROUP_TILES)
X_BUFS = 4
CHUNKS_OF_GROUP = (4, 4)
CHUNKS_OF_LAST_GROUP = (4, 2, 1, 1)


def chunk_list():
    chunks = []
    for g in range(GROUPS):
        first = 0
        for tiles in CHUNKS_OF_LAST_GROUP if g == GROUPS - 1 else CHUNKS_OF_GROUP:
            chunks.append((g, first, tiles))
            first += tiles
    return chunks


def tile_modelnew_t_kernel(
    tc, x, y, weight, bias, running_mean, running_var, norm_weight, norm_bias, out
):
    nc = tc.nc
    chunks = chunk_list()
    xv = x.rearrange("(g p t) k -> g p (t k)", p=P, t=GROUP_TILES)
    yv = y.rearrange("(g p t) f -> g p (t f)", p=P, t=GROUP_TILES)
    ov = out.rearrange("(g p t) f -> g p (t f)", p=P, t=GROUP_TILES)

    with ExitStack() as ctx:
        ctx.enter_context(tc.manual_schedule())
        const = ctx.enter_context(tc.tile_pool(name="const", bufs=1))
        xin = ctx.enter_context(tc.tile_pool(name="xin", bufs=X_BUFS))
        yin = ctx.enter_context(tc.tile_pool(name="yin", bufs=X_BUFS + 2))
        work = ctx.enter_context(tc.tile_pool(name="work", bufs=3))
        outp = ctx.enter_context(tc.tile_pool(name="outp", bufs=10))
        xtp = ctx.enter_context(tc.psum_pool(name="xtp", bufs=4))
        linp = ctx.enter_context(tc.psum_pool(name="linp", bufs=2))
        nbp = ctx.enter_context(tc.psum_pool(name="nbp", bufs=2))

        xs, ys = {}, {}
        grouped, codes, scales, products, norm_t, norm_b, results = {}, {}, {}, {}, {}, {}, {}

        def load_x(g, pieces):
            xs[g] = xin.tile([P, GROUP_TILES * IN_F], BF16, name="xs", tag="xs")
            w = GROUP_TILES * IN_F // pieces
            for s in range(pieces):
                nc.sync.dma_start(out=xs[g][:, s * w:(s + 1) * w], in_=xv[g][:, s * w:(s + 1) * w])

        def load_y(g):
            ys[g] = yin.tile([P, GROUP_TILES * OUT_F], BF16, name="ys", tag="ys")
            nc.sync.dma_start(out=ys[g][:], in_=yv[g])

        ident = const.tile([P, P], F32, name="ident")
        make_identity(nc, ident[:])
        vec_rows = const.tile([P, P], BF16, name="vec_rows")
        nc.vector.memset(vec_rows[:], 0.0)
        one = const.tile([P, 1], F32, name="one")
        nc.vector.memset(one[:], 1.0)
        for v, vec in enumerate((bias, running_mean, running_var, norm_weight, norm_bias)):
            nc.scalar.dma_start(
                out=vec_rows[HALVES * v:HALVES * (v + 1), :], in_=vec.rearrange("(h p) -> h p", h=HALVES)
            )
        root_of_one = const.tile([P, 1], F32, name="root_of_one")
        nc.scalar.sqrt(root_of_one[:], one[:])

        w_sb = const.tile([P, HALVES * IN_F], BF16, name="w_sb")
        nc.sync.dma_start(
            out=w_sb[:].rearrange("p (h k) -> p h k", h=HALVES),
            in_=weight.rearrange("(h p) k -> p h k", p=P),
        )
        load_x(0, 4)
        load_x(1, 2)
        load_y(0)
        for g in range(2, X_BUFS):
            load_x(g, 1)
            load_y(g - 1)

        def transpose_words(bank, words, tiles_of_words, c):
            for u in range(2):
                for n, t in enumerate(tiles_of_words):
                    w0 = 256 * c + P * u
                    nc.tensor.transpose(bank[:, u, n * P:(n + 1) * P], words[:, t, w0:w0 + P], ident[:])


        w_words = w_sb[:].bitcast(F32).rearrange("p (h w) -> p h w", h=HALVES)
        w_grouped = const.tile([P, PASSES * OUT_F * 4], BF16, name="w_grouped", align_bytes=64)
        w_grouped_words = w_grouped[:].bitcast(F32).rearrange("p (c f u) -> p c f u", c=PASSES, u=2)
        for c in range(PASSES):
            bank = xtp.tile([P, 2, 256], F32, name="wt", tag="xt")
            transpose_words(bank, w_words, range(HALVES), c)
            nc.vector.tensor_copy(out=w_grouped_words[:, c], in_=bank[:].rearrange("p u f -> p f u"))
        vec_rows32 = const.tile([P, P], F32, name="vec_rows32")
        nc.vector.tensor_copy(out=vec_rows32[:], in_=vec_rows[:])
        w_codes = const.tile([P, PASSES * OUT_F], U32, name="w_codes", align_bytes=64)
        w_scales = const.tile([P, PASSES * OUT_F], U8, name="w_scales", align_bytes=64)
        nc.vector.quantize_mx(out=w_codes[:].bitcast(FP8X4), scales=w_scales[:], in_=w_grouped[:])

        vec_cols_ps = nbp.tile([P, 2, 256], F32, name="vec_cols_ps", tag="nb")
        nc.tensor.transpose(vec_cols_ps[:, 0, 0:P], vec_rows32[:], ident[:])
        cols = const.tile([P, 5 * HALVES], F32, name="cols")
        nc.vector.tensor_copy(out=cols[:], in_=vec_cols_ps[:, 0, 0:5 * HALVES])
        bias_c, mean_c, var_c, gain_c, shift_c = [cols[:, HALVES * v:HALVES * (v + 1)] for v in range(5)]
        var_eps = const.tile([P, HALVES], F32, name="var_eps")
        std = const.tile([P, HALVES], F32, name="std")
        inv_std = const.tile([P, HALVES], F32, name="inv_std")
        centred = const.tile([P, HALVES], F32, name="centred")
        s_col = const.tile([P, HALVES], F32, name="s_col")
        t_col = const.tile([P, HALVES], F32, name="t_col")
        nc.vector.tensor_scalar_add(out=var_eps[:], in0=var_c, scalar1=EPS)
        nc.scalar.sqrt(std[:], var_eps[:])
        nc.vector.reciprocal(out=inv_std[:], in_=std[:])
        nc.vector.tensor_tensor(out=s_col[:], in0=inv_std[:], in1=gain_c, op=ALU.mult)
        nc.vector.tensor_tensor(out=centred[:], in0=bias_c, in1=mean_c, op=ALU.subtract)
        nc.vector.tensor_tensor(out=centred[:], in0=centred[:], in1=s_col[:], op=ALU.mult)
        nc.vector.tensor_tensor(out=t_col[:], in0=centred[:], in1=shift_c, op=ALU.add)


        def transpose_x(i):
            g, first, n = chunks[i]
            words = xs[g][:].bitcast(F32).rearrange("p (t w) -> p t w", t=GROUP_TILES)
            grouped[i] = work.tile([P, PASSES * 512 * 4], BF16, name="grouped", tag="grouped", align_bytes=64)
            grouped_words = (
                grouped[i][:, 0:PASSES * n * P * 4].bitcast(F32).rearrange("p (c r u) -> p c r u", c=PASSES, u=2)
            )
            for c in range(PASSES):
                for t0 in range(0, n, 2):
                    in_bank = min(2, n - t0)
                    bank = xtp.tile([P, 2, 256], F32, name="xt", tag="xt")
                    transpose_words(bank, words, range(first + t0, first + t0 + in_bank), c)
                    nc.scalar.copy(
                        out=grouped_words[:, c, t0 * P:(t0 + in_bank) * P, :],
                        in_=bank[:, :, 0:in_bank * P].rearrange("p u r -> p r u"),
                    )

        def quantise_x(i):
            n = chunks[i][2]
            codes[i] = work.tile([P, PASSES * 512], U32, name="codes", tag="codes", align_bytes=64)
            scales[i] = work.tile([P, PASSES * 512], U8, name="scales", tag="scales", align_bytes=64)
            for c in range(PASSES):
                r = slice(c * n * P, (c + 1) * n * P)
                nc.vector.quantize_mx(
                    out=codes[i][:, r].bitcast(FP8X4),
                    scales=scales[i][:, r],
                    in_=grouped[i][:, c * n * P * 4:(c + 1) * n * P * 4],
                )

        def multiply(i):
            n = chunks[i][2]
            products[i] = []
            for h in range(HALVES):
                acc = linp.tile([P, 512], F32, name="acc", tag="acc")
                for c in range(PASSES):
                    f = slice(c * OUT_F + h * P, c * OUT_F + (h + 1) * P)
                    r = slice(c * n * P, (c + 1) * n * P)
                    nc.tensor.matmul_mx(
                        out=acc[:, 0:n * P],
                        lhsT=w_codes[:, f].bitcast(FP8X4),
                        lhsT_scale=w_scales[:, f],
                        rhs=codes[i][:, r].bitcast(FP8X4),
                        rhs_scale=scales[i][:, r],
                        start=(c == 0),
                        stop=(c == PASSES - 1),
                    )
                products[i].append(acc)

        def normalise(i):
            n = chunks[i][2]
            norm_t[i] = work.tile([P, HALVES, 512], F32, name="norm_t", tag="norm_t")
            for h in range(HALVES):
                nc.scalar.activation(
                    out=norm_t[i][:, h, 0:n * P], in_=products[i][h][:, 0:n * P], func=ACT.Identity,
                    scale=s_col[:, h:h + 1], bias=t_col[:, h:h + 1],
                )

        def transpose_back(i):
            n = chunks[i][2]
            norm_b[i] = []
            for t in range(n):
                if t % 2 == 0:
                    norm_b[i].append(nbp.tile([P, 512], F32, name="nb", tag="nb"))
                for h in range(HALVES):
                    f0 = (t % 2) * OUT_F + h * P
                    nc.tensor.transpose(norm_b[i][-1][:, f0:f0 + P], norm_t[i][:, h, t * P:(t + 1) * P], ident[:])

        def finish(i):
            g, first, n = chunks[i]
            results[i] = outp.tile([P, 4 * OUT_F], F32, name="res", tag="res")
            res = results[i]
            half = n * OUT_F // 2
            y0 = first * OUT_F
            for q in range(2):
                lo = q * half
                nc.vector.tensor_tensor(
                    out=res[:, lo:lo + half],
                    in0=norm_b[i][lo // 512][:, lo % 512:lo % 512 + half],
                    in1=ys[g][:, y0 + lo:y0 + lo + half],
                    op=ALU.add,
                )
            for q in range(2):
                lo = q * half
                nc.vector.tensor_tensor(
                    out=res[:, lo:lo + half], in0=res[:, lo:lo + half], in1=ys[g][:, y0 + lo:y0 + lo + half],
                    op=ALU.mult,
                )
            nc.sync.dma_start(out=ov[g][:, y0:y0 + n * OUT_F], in_=res[:, 0:n * OUT_F])

        transpose_x(0)
        quantise_x(0)
        for k in range(len(chunks) + 1):
            if k + 1 < len(chunks):
                transpose_x(k + 1)
                g, first, n = chunks[k + 1]
                if first + n == GROUP_TILES and g + X_BUFS < GROUPS:
                    load_x(g + X_BUFS, 1)
                    load_y(g + X_BUFS - 1)
                    if g + X_BUFS == GROUPS - 1:
                        load_y(GROUPS - 1)
            if k < len(chunks):
                multiply(k)
                normalise(k)
            if k + 1 < len(chunks):
                quantise_x(k + 1)
            if k >= 1:
                transpose_back(k - 1)
                finish(k - 1)
